import numpy as np
import ml_dtypes


def mxq(x, axis, fmt="e4m3"):
    dtype, down = {"e4m3": (ml_dtypes.float8_e4m3fn, 7), "e5m2": (ml_dtypes.float8_e5m2, 14)}[fmt]
    v = np.moveaxis(np.asarray(x, np.float32).astype(ml_dtypes.bfloat16).astype(np.float64), axis, -1)
    blocks = v.reshape(v.shape[:-1] + (-1, 32))
    amax = np.abs(blocks).max(-1, keepdims=True)
    byte = np.maximum(np.where(amax > 0, np.frexp(amax)[1] - 1 + 127, 0) - down, 1)
    scale = np.exp2(byte - 127.0)
    codes = (blocks / scale).astype(np.float32).astype(dtype).astype(np.float64)
    return np.moveaxis((codes * scale).reshape(v.shape), -1, axis)


WIDE = False


def mx_kscale(k):
    if not WIDE:
        return np.ones(k)
    levels = np.array([10, -10, 5, -5, 0])
    a = np.random.permutation(np.resize(levels, k // 512 * 4)).reshape(k // 512, 4)
    idx = np.arange(k)
    return np.exp2(a[idx // 512, idx % 128 // 32])


BF16 = ml_dtypes.bfloat16


def bf(x):
    return np.asarray(x, np.float32).astype(BF16)


def f64(x):
    return np.asarray(x).astype(np.float64)


E2M1 = np.array([0.0, 0.5, 1.0, 1.5, 2.0, 3.0, 4.0, 6.0, -0.0, -0.5, -1.0, -1.5, -2.0, -3.0, -4.0, -6.0])


def pack_weight(w, fmt):
    k, n = w.shape
    w = f64(bf(w)).reshape(k // 32, 32, n)
    amax = np.abs(w).max(1)
    if fmt == "e4m3":
        byte = np.frexp(amax)[1] - 1 + 127 - 7
    else:
        mant, ex = np.frexp(amax / 6.0)
        byte = np.where(mant > 0.5, ex, ex - 1) + 127
    byte = np.clip(np.where(amax > 0, byte, 1), 1, 254)
    scaled = (w * np.exp2(127.0 - byte)[:, None, :]).reshape(k, n).astype(np.float32)
    by_word = np.ascontiguousarray(scaled.reshape(k // 512, 128, 4, n).transpose(0, 1, 3, 2))
    if fmt == "e4m3":
        words = by_word.astype(ml_dtypes.float8_e4m3fn).view(np.uint8)
    else:
        c = by_word.astype(ml_dtypes.float4_e2m1fn).view(np.uint8) & 0xF
        words = c[..., 0::2] | (c[..., 1::2] << 4)
    return np.ascontiguousarray(words), np.ascontiguousarray(byte.astype(np.uint8).reshape(k // 512, 16, n))


def unpack_weight(words, scales, fmt):
    g, p, n, _ = words.shape
    if fmt == "e4m3":
        vals = np.ascontiguousarray(words).view(ml_dtypes.float8_e4m3fn).astype(np.float64)
    else:
        nib = np.empty((g, p, n, 4), np.uint8)
        nib[..., 0::2] = words & 0xF
        nib[..., 1::2] = words >> 4
        vals = E2M1[nib]
    vals = vals * np.repeat(np.exp2(scales.astype(np.float64) - 127.0), 8, axis=1)[..., None]
    return vals.transpose(0, 1, 3, 2).reshape(g * 512, n)


B, I, N, M = 512, 512, 512, 4
K = I + N
NM = N * M
FMT = "e4m3"


def sigmoid(v):
    return 1.0 / (1.0 + np.exp(-v))


def softmax(v):
    e = np.exp(v - v.max())
    return e / e.sum()


def setup_inputs():
    s = mx_kscale(K)[:I]
    d = np.concatenate([s, np.ones(N)])[:, None]
    inputs = bf(np.random.standard_normal((B, I)) * s)
    state = bf(np.random.standard_normal((B, NM)) / np.sqrt(M))
    W_z_words, W_z_scales = pack_weight(np.random.standard_normal((K, NM)) / np.sqrt(K) / d, FMT)
    b_z = bf(np.random.standard_normal(NM) * 0.1)
    W_r_words, W_r_scales = pack_weight(np.random.standard_normal((K, NM)) / np.sqrt(K) / d, FMT)
    b_r = bf(np.random.standard_normal(NM) * 0.1)
    W_h_words, W_h_scales = pack_weight(np.random.standard_normal((K, NM)) / np.sqrt(K) / d, FMT)
    b_h = bf(np.random.standard_normal(NM) * 0.1)
    return {'inputs': inputs,
            'state': state,
            'W_z_words': W_z_words,
            'W_z_scales': W_z_scales,
            'b_z': b_z,
            'W_r_words': W_r_words,
            'W_r_scales': W_r_scales,
            'b_r': b_r,
            'W_h_words': W_h_words,
            'W_h_scales': W_h_scales,
            'b_h': b_h}


def reference(inputs, state, W_z_words, W_z_scales, b_z, W_r_words, W_r_scales, b_r, W_h_words, W_h_scales, b_h):
    x = f64(inputs)
    Wz = unpack_weight(W_z_words, W_z_scales, FMT)
    Wr = unpack_weight(W_r_words, W_r_scales, FMT)
    Wh = unpack_weight(W_h_words, W_h_scales, FMT)
    Bb, input_size = x.shape
    n = Wz.shape[0] - input_size
    m = Wz.shape[1] // n
    ln_tau = 0.5 * np.log(10.0) * np.arange(m, dtype=np.float64)
    alpha = softmax(-ln_tau)
    h = f64(state).reshape(Bb, n, m)
    h_sum = h.sum(axis=2)
    fq = mxq(np.concatenate([x, h_sum], axis=-1), 1, 'e4m3')
    z = sigmoid((fq @ Wz) + f64(b_z)).reshape(Bb, n, m)
    r = sigmoid((fq @ Wr) + f64(b_r)).reshape(Bb, n, m)
    r_h = (r * h).sum(axis=2)
    frq = mxq(np.concatenate([x, r_h], axis=-1), 1, 'e4m3')
    h_hat = np.tanh((frq @ Wh) + f64(b_h)).reshape(Bb, n, m)
    h_new = (1.0 - z) * h + z * alpha * h_hat
    output = h_new.sum(axis=2)
    new_state = h_new.reshape(Bb, n * m)
    return output, new_state

@@ -1,0 +1,323 @@
+import math
+from contextlib import ExitStack
+
+import concourse.mybir as mybir
+from concourse.masks import make_identity
+
+F32 = mybir.dt.float32
+BF16 = mybir.dt.bfloat16
+I32 = mybir.dt.int32
+U32 = mybir.dt.uint32
+U8 = mybir.dt.uint8
+FP8X4 = mybir.dt.float8_e4m3fn_x4
+ACT = mybir.ActivationFunctionType
+ALU = mybir.AluOpType
+AXIS = mybir.AxisListType
+
+P = 128
+BATCH = 512
+UNITS = 512
+SCALES = 4
+COLS = UNITS * SCALES
+PACK = 4
+K_PASS = P * PACK
+PASSES = 2
+B_TILES = BATCH // P
+COL_TILES = COLS // P
+TILE_UNITS = P // SCALES
+GROUP = 4
+HALF_TILES = COL_TILES // 2
+LAG = 5
+RH_READY = LAG + 2
+
+FLOPS = 3 * 2 * BATCH * PASSES * K_PASS * COLS
+
+DECAY = [math.exp(-0.5 * math.log(10.0) * m) for m in range(SCALES)]
+ALPHA = [d / sum(DECAY) for d in DECAY]
+
+R, Z, H = 0, 1, 2
+X, H_SUM, R_H = 0, 1, 2
+
+
+def tile_ctgrucell_kernel(
+    tc,
+    inputs,
+    state,
+    W_z_words,
+    W_z_scales,
+    b_z,
+    W_r_words,
+    W_r_scales,
+    b_r,
+    W_h_words,
+    W_h_scales,
+    b_h,
+    out_0,
+    out_1,
+):
+    nc = tc.nc
+    with ExitStack() as stack:
+        const = stack.enter_context(tc.tile_pool(name="const", bufs=1))
+        keep = stack.enter_context(tc.tile_pool(name="keep", bufs=1))
+        work = stack.enter_context(tc.tile_pool(name="work", bufs=3))
+        psum_acc = stack.enter_context(tc.psum_pool(name="psum_acc", bufs=3))
+        psum_turn = stack.enter_context(tc.psum_pool(name="psum_turn", bufs=3))
+        psum_sum = stack.enter_context(tc.psum_pool(name="psum_sum", bufs=2))
+        stack.enter_context(tc.manual_schedule())
+
+        planes = keep.tile([P, 2, COLS], U8, align_bytes=64)
+        nc.vector.memset(planes[:].bitcast(I32), 0)
+        bias_rows = const.tile([P, P], BF16)
+        nc.vector.memset(bias_rows[:], 0.0)
+        ones = const.tile([P, TILE_UNITS, SCALES], F32)
+        nc.vector.memset(ones[:], 1.0)
+        alpha_rows = const.tile([P, TILE_UNITS, SCALES], F32)
+        for m in range(SCALES):
+            nc.vector.tensor_scalar_mul(out=alpha_rows[:, :, m], in0=ones[:, :, m], scalar1=ALPHA[m])
+        ident_f32 = const.tile([P, P], F32)
+        make_identity(nc, ident_f32[:])
+        table_warmer = const.tile([P, 1], F32)
+        nc.scalar.activation(out=table_warmer[:], in_=ones[:, 0, 0:1], func=ACT.Sigmoid)
+
+        x_nat = keep.tile([P, B_TILES, K_PASS], BF16)
+        nc.sync.dma_start(out=x_nat[:], in_=inputs.rearrange("(i b) k -> b i k", b=P))
+        h_nat = [keep.tile([P, COLS], BF16, name="h_nat%d" % i) for i in range(B_TILES)]
+        for i in range(B_TILES):
+            nc.sync.dma_start(out=h_nat[i][:], in_=state[i * P : (i + 1) * P, :])
+
+        def plane_start(gate, g):
+            return 8 * (gate % 2) + 4 * g
+
+        def load_scales(gate, scales):
+            for quadrant in range(4):
+                first = 32 * quadrant + plane_start(gate, 0)
+                nc.sync.dma_start(
+                    out=planes[first : first + 4 * PASSES, gate // 2, :].bitcast(I32),
+                    in_=scales[:, 4 * quadrant : 4 * quadrant + 4, :].bitcast(I32),
+                )
+
+        def load_words(gate, words):
+            halves = []
+            for half in range(2):
+                cols = slice(half * HALF_TILES * P, (half + 1) * HALF_TILES * P)
+                part = keep.tile(
+                    [P, PASSES, HALF_TILES * P], U32, name="words%d_%d" % (gate, half), align_bytes=64
+                )
+                nc.sync.dma_start(
+                    out=part[:].bitcast(I32),
+                    in_=words[:, :, cols, :].rearrange("g p c t -> p g (c t)").bitcast(I32),
+                )
+                halves.append(part)
+            return halves
+
+        w_words = {}
+        load_scales(R, W_r_scales)
+        w_words[R] = load_words(R, W_r_words)
+        load_scales(Z, W_z_scales)
+        load_scales(H, W_h_scales)
+        w_words[Z] = load_words(Z, W_z_words)
+        w_words[H] = load_words(H, W_h_words)
+        for gate, b in ((R, b_r), (Z, b_z), (H, b_h)):
+            nc.scalar.dma_start(
+                out=bias_rows[gate * COL_TILES : (gate + 1) * COL_TILES, :],
+                in_=b.rearrange("(j c) -> j c", c=P),
+            )
+
+        ident_bf = const.tile([P, P], BF16)
+        nc.vector.tensor_copy(out=ident_bf[:], in_=ident_f32[:])
+        sum4 = const.tile([P, TILE_UNITS], F32)
+        nc.vector.tensor_reduce(
+            out=sum4[:],
+            in_=ident_f32[:].rearrange("c (n m) -> c n m", m=SCALES),
+            axis=AXIS.X,
+            op=ALU.add,
+        )
+        alpha_turned = psum_turn.tile([P, P], F32, tag="turn")
+        nc.tensor.transpose(alpha_turned[:], alpha_rows[:].rearrange("p n m -> p (n m)"), ident_f32[:])
+        alpha_col = const.tile([P, 1], F32)
+        nc.vector.tensor_copy(out=alpha_col[:], in_=alpha_turned[:, 0:1])
+
+        act_codes = keep.tile([P, 3, BATCH], U32, align_bytes=64)
+        act_scales = keep.tile([P, 3, BATCH], U8, align_bytes=64)
+
+        def group_rows(sorted_nat, grouped, i, copy_out):
+            turned = psum_turn.tile([P, PACK, P], BF16, tag="turn")
+            for t in range(PACK):
+                nc.tensor.transpose(turned[:, t, :], sorted_nat[:, i, t, :], ident_bf[:])
+            copy_out(out=grouped[:, i * P : (i + 1) * P, :], in_=turned[:].rearrange("p t b -> p b t"))
+
+        def either_engine(i):
+            return nc.vector.tensor_copy if i % 2 else nc.scalar.copy
+
+        def quantise(grouped, slot):
+            nc.vector.quantize_mx(
+                out=act_codes[:, slot, :].bitcast(FP8X4),
+                scales=act_scales[:, slot, :],
+                in_=grouped[:].rearrange("p b t -> p (b t)"),
+            )
+
+        x_sorted = keep.tile([P, B_TILES, PACK, P], BF16)
+        nc.vector.tensor_copy(out=x_sorted[:], in_=x_nat[:].rearrange("b i (p t) -> b i t p", t=PACK))
+        x_grouped = work.tile([P, BATCH, PACK], BF16, tag="grouped", bufs=2, align_bytes=64)
+        for i in range(B_TILES):
+            group_rows(x_sorted, x_grouped, i, nc.scalar.copy)
+
+        h_turned = keep.tile([P, COL_TILES, BATCH], BF16)
+        hsum_sorted = keep.tile([P, B_TILES, PACK, P], BF16)
+        for i in range(B_TILES):
+            with nc.allow_low_precision(reason="h_sum is rounded once to bfloat16, as the task says"):
+                nc.vector.tensor_reduce(
+                    out=hsum_sorted[:, i, :, :],
+                    in_=h_nat[i][:].rearrange("b (p t m) -> b t p m", t=PACK, m=SCALES),
+                    axis=AXIS.X,
+                    op=ALU.add,
+                )
+            for quarter in range(COL_TILES // GROUP):
+                turned = psum_turn.tile([P, GROUP, P], BF16, tag="turn")
+                for jj in range(GROUP):
+                    j = quarter * GROUP + jj
+                    nc.tensor.transpose(turned[:, jj, :], h_nat[i][:, j * P : (j + 1) * P], ident_bf[:])
+                nc.scalar.copy(
+                    out=h_turned[:, quarter * GROUP : (quarter + 1) * GROUP, i * P : (i + 1) * P],
+                    in_=turned[:],
+                )
+        quantise(x_grouped, X)
+
+        bias_turned = psum_turn.tile([P, P], BF16, tag="turn")
+        nc.tensor.transpose(bias_turned[:], bias_rows[:], ident_bf[:])
+        bias = const.tile([P, P], F32)
+        nc.vector.tensor_copy(out=bias[:], in_=bias_turned[:])
+
+        hsum_grouped = work.tile([P, BATCH, PACK], BF16, tag="grouped", bufs=2, align_bytes=64)
+        for i in range(B_TILES):
+            group_rows(hsum_sorted, hsum_grouped, i, either_engine(i))
+        quantise(hsum_grouped, H_SUM)
+
+        def gate_tile(gate, j, state_slot):
+            acc = psum_acc.tile([P, BATCH], F32, tag="acc")
+            part = w_words[gate][j // HALF_TILES]
+            cols = slice((j % HALF_TILES) * P, (j % HALF_TILES + 1) * P)
+            for g, slot in enumerate((X, state_slot)):
+                nc.tensor.matmul_mx(
+                    out=acc[:],
+                    lhsT=part[:, g, cols].bitcast(FP8X4),
+                    lhsT_scale=planes[plane_start(gate, g) : P, gate // 2, j * P : (j + 1) * P],
+                    rhs=act_codes[:, slot, :].bitcast(FP8X4),
+                    rhs_scale=act_scales[:, slot, :],
+                    start=(g == 0),
+                    stop=(g == PASSES - 1),
+                )
+            return acc
+
+        def bias_of(gate, j):
+            return bias[:, gate * COL_TILES + j : gate * COL_TILES + j + 1]
+
+        def sum_scales(sums, j, turned):
+            at = (j % GROUP) * TILE_UNITS
+            for i in range(B_TILES):
+                nc.tensor.matmul(
+                    out=sums[:, i, at : at + TILE_UNITS],
+                    lhsT=turned[:, i * P : (i + 1) * P],
+                    rhs=sum4[:],
+                    start=True,
+                    stop=True,
+                )
+
+        rh_sorted = keep.tile([P, B_TILES, PACK, P], BF16)
+        rh = {}
+        rh_sums = {}
+
+        def reset_gate(j):
+            acc = gate_tile(R, j, H_SUM)
+            r = work.tile([P, BATCH], F32, tag="gate")
+            nc.scalar.activation(out=r[:], in_=acc[:], func=ACT.Sigmoid, bias=bias_of(R, j), scale=1.0)
+            rh[j] = work.tile([P, BATCH], F32, name="rh", tag="lagged", bufs=LAG + 2)
+            nc.vector.tensor_mul(out=rh[j][:], in0=r[:], in1=h_turned[:, j, :])
+
+        def sum_rh(j):
+            group = j // GROUP
+            if j % GROUP == 0:
+                rh_sums[group] = psum_sum.tile(
+                    [P, B_TILES, GROUP * TILE_UNITS], F32, name="rh_sums", tag="sum"
+                )
+            sum_scales(rh_sums[group], j, rh[j])
+            if j % GROUP == GROUP - 1:
+                nc.vector.tensor_copy(
+                    out=rh_sorted[:, :, :, group * TILE_UNITS : (group + 1) * TILE_UNITS],
+                    in_=rh_sums[group][:].rearrange("b i (p t) -> b i t p", t=PACK),
+                )
+
+        for j in range(COL_TILES):
+            reset_gate(j)
+            if j >= LAG:
+                sum_rh(j - LAG)
+
+        z = [keep.tile([P, BATCH], F32, name="z%d" % j) for j in range(COL_TILES)]
+        minus_kept = [keep.tile([P, BATCH], F32, name="minus_kept%d" % j) for j in range(COL_TILES)]
+        for j in range(COL_TILES):
+            acc = gate_tile(Z, j, H_SUM)
+            nc.scalar.activation(out=z[j][:], in_=acc[:], func=ACT.Sigmoid, bias=bias_of(Z, j), scale=1.0)
+            nc.vector.scalar_tensor_tensor(
+                out=minus_kept[j][:],
+                in0=z[j][:],
+                scalar=1.0,
+                in1=h_turned[:, j, :],
+                op0=ALU.subtract,
+                op1=ALU.mult,
+            )
+            if j < LAG:
+                sum_rh(COL_TILES - LAG + j)
+            if j == RH_READY:
+                rh_grouped = work.tile([P, BATCH, PACK], BF16, tag="grouped", bufs=2, align_bytes=64)
+                for i in range(B_TILES):
+                    group_rows(rh_sorted, rh_grouped, i, either_engine(i))
+                quantise(rh_grouped, R_H)
+
+        new_state = out_1.rearrange("(i b) c -> b i c", b=P)
+        output = out_0.rearrange("(i b) n -> b i n", b=P)
+        h_new = {}
+        out_sums = {}
+
+        def blend(j):
+            acc = gate_tile(H, j, R_H)
+            h_hat = work.tile([P, BATCH], F32, tag="gate")
+            nc.scalar.activation(out=h_hat[:], in_=acc[:], func=ACT.Tanh, bias=bias_of(H, j), scale=1.0)
+            fresh = work.tile([P, BATCH], F32, tag="fresh")
+            nc.vector.scalar_tensor_tensor(
+                out=fresh[:],
+                in0=z[j][:],
+                scalar=alpha_col[:, 0:1],
+                in1=h_hat[:],
+                op0=ALU.mult,
+                op1=ALU.mult,
+            )
+            h_new[j] = work.tile([P, BATCH], F32, name="h_new", tag="lagged", bufs=LAG + 2)
+            nc.vector.tensor_sub(out=h_new[j][:], in0=fresh[:], in1=minus_kept[j][:])
+
+        def send_back(j):
+            back = psum_turn.tile([P, B_TILES, P], F32, tag="turn")
+            for i in range(B_TILES):
+                nc.tensor.transpose(back[:, i, :], h_new[j][:, i * P : (i + 1) * P], ident_f32[:])
+            state_out = work.tile([P, B_TILES, P], F32, tag="state_out")
+            nc.scalar.copy(out=state_out[:], in_=back[:])
+            nc.sync.dma_start(out=new_state[:, :, j * P : (j + 1) * P], in_=state_out[:])
+            group = j // GROUP
+            if j % GROUP == 0:
+                out_sums[group] = psum_sum.tile(
+                    [P, B_TILES, GROUP * TILE_UNITS], F32, name="out_sums", tag="sum"
+                )
+            sum_scales(out_sums[group], j, h_new[j])
+            if j % GROUP == GROUP - 1:
+                output_out = work.tile([P, B_TILES, GROUP * TILE_UNITS], F32, tag="output_out", bufs=2)
+                nc.vector.tensor_copy(out=output_out[:], in_=out_sums[group][:])
+                nc.sync.dma_start(
+                    out=output[:, :, group * GROUP * TILE_UNITS : (group + 1) * GROUP * TILE_UNITS],
+                    in_=output_out[:],
+                )
+
+        for j in range(COL_TILES):
+            blend(j)
+            if j >= LAG:
+                send_back(j - LAG)
+        for j in range(COL_TILES - LAG, COL_TILES):
+            send_back(j)

@@ -27,8 +27,8 @@ COL_TILES = COLS // P
 TILE_UNITS = P // SCALES
 GROUP = 4
 HALF_TILES = COL_TILES // 2
-LAG = 5
-RH_READY = LAG + 2
+LAG = 3
+RH_READY = LAG + 1
 
 FLOPS = 3 * 2 * BATCH * PASSES * K_PASS * COLS
 
@@ -60,9 +60,8 @@ def tile_ctgrucell_kernel(
         const = stack.enter_context(tc.tile_pool(name="const", bufs=1))
         keep = stack.enter_context(tc.tile_pool(name="keep", bufs=1))
         work = stack.enter_context(tc.tile_pool(name="work", bufs=3))
-        psum_acc = stack.enter_context(tc.psum_pool(name="psum_acc", bufs=3))
-        psum_turn = stack.enter_context(tc.psum_pool(name="psum_turn", bufs=3))
-        psum_sum = stack.enter_context(tc.psum_pool(name="psum_sum", bufs=2))
+        psum_acc = stack.enter_context(tc.psum_pool(name="psum_acc", bufs=4))
+        psum_turn = stack.enter_context(tc.psum_pool(name="psum_turn", bufs=4))
         stack.enter_context(tc.manual_schedule())
 
         planes = keep.tile([P, 2, COLS], U8, align_bytes=64)
@@ -73,16 +72,17 @@ def tile_ctgrucell_kernel(
         nc.vector.memset(ones[:], 1.0)
         alpha_rows = const.tile([P, TILE_UNITS, SCALES], F32)
         for m in range(SCALES):
-            nc.vector.tensor_scalar_mul(out=alpha_rows[:, :, m], in0=ones[:, :, m], scalar1=ALPHA[m])
+            nc.vector.tensor_scalar_mul(out=alpha_rows[:, :, m], in0=ones[:, :, m], scalar1=-ALPHA[m])
         ident_f32 = const.tile([P, P], F32)
         make_identity(nc, ident_f32[:])
         table_warmer = const.tile([P, 1], F32)
         nc.scalar.activation(out=table_warmer[:], in_=ones[:, 0, 0:1], func=ACT.Sigmoid)
 
         x_nat = keep.tile([P, B_TILES, K_PASS], BF16)
-        nc.sync.dma_start(out=x_nat[:], in_=inputs.rearrange("(i b) k -> b i k", b=P))
         h_nat = [keep.tile([P, COLS], BF16, name="h_nat%d" % i) for i in range(B_TILES)]
         for i in range(B_TILES):
+            if i == B_TILES // 2:
+                nc.sync.dma_start(out=x_nat[:], in_=inputs.rearrange("(i b) k -> b i k", b=P))
             nc.sync.dma_start(out=h_nat[i][:], in_=state[i * P : (i + 1) * P, :])
 
         def plane_start(gate, g):
@@ -125,26 +125,27 @@ def tile_ctgrucell_kernel(
 
         ident_bf = const.tile([P, P], BF16)
         nc.vector.tensor_copy(out=ident_bf[:], in_=ident_f32[:])
-        sum4 = const.tile([P, TILE_UNITS], F32)
-        nc.vector.tensor_reduce(
-            out=sum4[:],
-            in_=ident_f32[:].rearrange("c (n m) -> c n m", m=SCALES),
-            axis=AXIS.X,
-            op=ALU.add,
-        )
         alpha_turned = psum_turn.tile([P, P], F32, tag="turn")
         nc.tensor.transpose(alpha_turned[:], alpha_rows[:].rearrange("p n m -> p (n m)"), ident_f32[:])
-        alpha_col = const.tile([P, 1], F32)
-        nc.vector.tensor_copy(out=alpha_col[:], in_=alpha_turned[:, 0:1])
+        minus_alpha = const.tile([P, 1], F32)
+        nc.vector.tensor_copy(out=minus_alpha[:], in_=alpha_turned[:, 0:1])
 
         act_codes = keep.tile([P, 3, BATCH], U32, align_bytes=64)
         act_scales = keep.tile([P, 3, BATCH], U8, align_bytes=64)
 
-        def group_rows(sorted_nat, grouped, i, copy_out):
-            turned = psum_turn.tile([P, PACK, P], BF16, tag="turn")
-            for t in range(PACK):
-                nc.tensor.transpose(turned[:, t, :], sorted_nat[:, i, t, :], ident_bf[:])
-            copy_out(out=grouped[:, i * P : (i + 1) * P, :], in_=turned[:].rearrange("p t b -> p b t"))
+        def group_rows(planes, grouped_rows, ident, copy_out):
+            turned = psum_turn.tile([P, len(planes), P], ident.dtype, tag="turn")
+            for k in range(len(planes)):
+                nc.tensor.transpose(turned[:, k, :], planes[k], ident)
+            copy_out(out=grouped_rows, in_=turned[:].rearrange("p k b -> p b k"))
+
+        def group_sorted(sorted_nat, grouped, i, copy_out):
+            group_rows(
+                [sorted_nat[:, i, t, :] for t in range(PACK)],
+                grouped[:, i * P : (i + 1) * P, :],
+                ident_bf[:],
+                copy_out,
+            )
 
         def either_engine(i):
             return nc.vector.tensor_copy if i % 2 else nc.scalar.copy
@@ -156,13 +157,6 @@ def tile_ctgrucell_kernel(
                 in_=grouped[:].rearrange("p b t -> p (b t)"),
             )
 
-        x_sorted = keep.tile([P, B_TILES, PACK, P], BF16)
-        nc.vector.tensor_copy(out=x_sorted[:], in_=x_nat[:].rearrange("b i (p t) -> b i t p", t=PACK))
-        x_grouped = work.tile([P, BATCH, PACK], BF16, tag="grouped", bufs=2, align_bytes=64)
-        for i in range(B_TILES):
-            group_rows(x_sorted, x_grouped, i, nc.scalar.copy)
-
-        h_turned = keep.tile([P, COL_TILES, BATCH], BF16)
         hsum_sorted = keep.tile([P, B_TILES, PACK, P], BF16)
         for i in range(B_TILES):
             with nc.allow_low_precision(reason="h_sum is rounded once to bfloat16, as the task says"):
@@ -172,26 +166,47 @@ def tile_ctgrucell_kernel(
                     axis=AXIS.X,
                     op=ALU.add,
                 )
+
+        h_turned = keep.tile([P, COL_TILES, BATCH], BF16)
+
+        def turn_state(i, copy_out):
             for quarter in range(COL_TILES // GROUP):
                 turned = psum_turn.tile([P, GROUP, P], BF16, tag="turn")
                 for jj in range(GROUP):
                     j = quarter * GROUP + jj
                     nc.tensor.transpose(turned[:, jj, :], h_nat[i][:, j * P : (j + 1) * P], ident_bf[:])
-                nc.scalar.copy(
+                copy_out(
                     out=h_turned[:, quarter * GROUP : (quarter + 1) * GROUP, i * P : (i + 1) * P],
                     in_=turned[:],
                 )
-        quantise(x_grouped, X)
 
+        turn_state(0, nc.scalar.copy)
         bias_turned = psum_turn.tile([P, P], BF16, tag="turn")
         nc.tensor.transpose(bias_turned[:], bias_rows[:], ident_bf[:])
         bias = const.tile([P, P], F32)
-        nc.vector.tensor_copy(out=bias[:], in_=bias_turned[:])
+        nc.scalar.copy(out=bias[:], in_=bias_turned[:])
+        turn_state(1, nc.scalar.copy)
+
+        x_grouped = work.tile([P, BATCH, PACK], BF16, tag="grouped", bufs=2, align_bytes=64)
+        x_grouped_words = (
+            x_grouped[:].rearrange("p b t -> p (b t)").bitcast(F32).rearrange("p (b u) -> p b u", u=2)
+        )
+        for i in range(B_TILES):
+            x_words = x_nat[:, i, :].bitcast(F32)
+            group_rows(
+                [x_words[:, u : K_PASS // 2 : 2] for u in range(2)],
+                x_grouped_words[:, i * P : (i + 1) * P, :],
+                ident_f32[:],
+                nc.scalar.copy,
+            )
+        quantise(x_grouped, X)
+        turn_state(2, nc.scalar.copy)
 
         hsum_grouped = work.tile([P, BATCH, PACK], BF16, tag="grouped", bufs=2, align_bytes=64)
         for i in range(B_TILES):
-            group_rows(hsum_sorted, hsum_grouped, i, either_engine(i))
+            group_sorted(hsum_sorted, hsum_grouped, i, nc.scalar.copy)
         quantise(hsum_grouped, H_SUM)
+        turn_state(3, nc.vector.tensor_copy)
 
         def gate_tile(gate, j, state_slot):
             acc = psum_acc.tile([P, BATCH], F32, tag="acc")
@@ -212,20 +227,8 @@ def tile_ctgrucell_kernel(
         def bias_of(gate, j):
             return bias[:, gate * COL_TILES + j : gate * COL_TILES + j + 1]
 
-        def sum_scales(sums, j, turned):
-            at = (j % GROUP) * TILE_UNITS
-            for i in range(B_TILES):
-                nc.tensor.matmul(
-                    out=sums[:, i, at : at + TILE_UNITS],
-                    lhsT=turned[:, i * P : (i + 1) * P],
-                    rhs=sum4[:],
-                    start=True,
-                    stop=True,
-                )
-
         rh_sorted = keep.tile([P, B_TILES, PACK, P], BF16)
         rh = {}
-        rh_sums = {}
 
         def reset_gate(j):
             acc = gate_tile(R, j, H_SUM)
@@ -235,16 +238,16 @@ def tile_ctgrucell_kernel(
             nc.vector.tensor_mul(out=rh[j][:], in0=r[:], in1=h_turned[:, j, :])
 
         def sum_rh(j):
-            group = j // GROUP
-            if j % GROUP == 0:
-                rh_sums[group] = psum_sum.tile(
-                    [P, B_TILES, GROUP * TILE_UNITS], F32, name="rh_sums", tag="sum"
-                )
-            sum_scales(rh_sums[group], j, rh[j])
-            if j % GROUP == GROUP - 1:
-                nc.vector.tensor_copy(
-                    out=rh_sorted[:, :, :, group * TILE_UNITS : (group + 1) * TILE_UNITS],
-                    in_=rh_sums[group][:].rearrange("b i (p t) -> b i t p", t=PACK),
+            back = psum_turn.tile([P, B_TILES, P], F32, tag="turn")
+            for i in range(B_TILES):
+                nc.tensor.transpose(back[:, i, :], rh[j][:, i * P : (i + 1) * P], ident_f32[:])
+            units = TILE_UNITS // PACK
+            with nc.allow_low_precision(reason="r_h is rounded once to bfloat16, as the task says"):
+                nc.vector.tensor_reduce(
+                    out=rh_sorted[:, :, :, j * units : (j + 1) * units],
+                    in_=back[:].rearrange("b i (q t m) -> b i t q m", t=PACK, m=SCALES),
+                    axis=AXIS.X,
+                    op=ALU.add,
                 )
 
         for j in range(COL_TILES):
@@ -270,53 +273,63 @@ def tile_ctgrucell_kernel(
             if j == RH_READY:
                 rh_grouped = work.tile([P, BATCH, PACK], BF16, tag="grouped", bufs=2, align_bytes=64)
                 for i in range(B_TILES):
-                    group_rows(rh_sorted, rh_grouped, i, either_engine(i))
+                    group_sorted(rh_sorted, rh_grouped, i, either_engine(i))
                 quantise(rh_grouped, R_H)
 
         new_state = out_1.rearrange("(i b) c -> b i c", b=P)
         output = out_0.rearrange("(i b) n -> b i n", b=P)
-        h_new = {}
-        out_sums = {}
+        minus_fresh = {}
+        output_out = {}
 
-        def blend(j):
+        def candidate(j):
             acc = gate_tile(H, j, R_H)
             h_hat = work.tile([P, BATCH], F32, tag="gate")
             nc.scalar.activation(out=h_hat[:], in_=acc[:], func=ACT.Tanh, bias=bias_of(H, j), scale=1.0)
-            fresh = work.tile([P, BATCH], F32, tag="fresh")
+            minus_fresh[j] = work.tile([P, BATCH], F32, name="minus_fresh", tag="lagged", bufs=LAG + 2)
             nc.vector.scalar_tensor_tensor(
-                out=fresh[:],
+                out=minus_fresh[j][:],
                 in0=z[j][:],
-                scalar=alpha_col[:, 0:1],
+                scalar=minus_alpha[:, 0:1],
                 in1=h_hat[:],
                 op0=ALU.mult,
                 op1=ALU.mult,
             )
-            h_new[j] = work.tile([P, BATCH], F32, name="h_new", tag="lagged", bufs=LAG + 2)
-            nc.vector.tensor_sub(out=h_new[j][:], in0=fresh[:], in1=minus_kept[j][:])
 
         def send_back(j):
             back = psum_turn.tile([P, B_TILES, P], F32, tag="turn")
             for i in range(B_TILES):
-                nc.tensor.transpose(back[:, i, :], h_new[j][:, i * P : (i + 1) * P], ident_f32[:])
+                rows = slice(i * P, (i + 1) * P)
+                nc.tensor.matmul(
+                    out=back[:, i, :], lhsT=minus_kept[j][:, rows], rhs=ident_f32[:],
+                    is_transpose=True, start=True, stop=False,
+                )
+                nc.tensor.matmul(
+                    out=back[:, i, :], lhsT=minus_fresh[j][:, rows], rhs=ident_f32[:],
+                    is_transpose=True, start=False, stop=True,
+                )
             state_out = work.tile([P, B_TILES, P], F32, tag="state_out")
-            nc.scalar.copy(out=state_out[:], in_=back[:])
+            nc.scalar.mul(out=state_out[:], in_=back[:], mul=-1.0)
             nc.sync.dma_start(out=new_state[:, :, j * P : (j + 1) * P], in_=state_out[:])
             group = j // GROUP
             if j % GROUP == 0:
-                out_sums[group] = psum_sum.tile(
-                    [P, B_TILES, GROUP * TILE_UNITS], F32, name="out_sums", tag="sum"
+                output_out[group] = work.tile(
+                    [P, B_TILES, GROUP * TILE_UNITS], F32, name="output_out", tag="output_out", bufs=2
                 )
-            sum_scales(out_sums[group], j, h_new[j])
+            at = (j % GROUP) * TILE_UNITS
+            nc.vector.tensor_reduce(
+                out=output_out[group][:, :, at : at + TILE_UNITS],
+                in_=state_out[:].rearrange("b i (n m) -> b i n m", m=SCALES),
+                axis=AXIS.X,
+                op=ALU.add,
+            )
             if j % GROUP == GROUP - 1:
-                output_out = work.tile([P, B_TILES, GROUP * TILE_UNITS], F32, tag="output_out", bufs=2)
-                nc.vector.tensor_copy(out=output_out[:], in_=out_sums[group][:])
                 nc.sync.dma_start(
                     out=output[:, :, group * GROUP * TILE_UNITS : (group + 1) * GROUP * TILE_UNITS],
-                    in_=output_out[:],
+                    in_=output_out[group][:],
                 )
 
         for j in range(COL_TILES):
-            blend(j)
+            candidate(j)
             if j >= LAG:
                 send_back(j - LAG)
         for j in range(COL_TILES - LAG, COL_TILES):

@@ -27,8 +27,10 @@ COL_TILES = COLS // P
 TILE_UNITS = P // SCALES
 GROUP = 4
 HALF_TILES = COL_TILES // 2
-LAG = 3
-RH_READY = LAG + 1
+RUN = 2
+RUNS = COL_TILES // RUN
+LAG = 2
+RH_READY = LAG
 
 FLOPS = 3 * 2 * BATCH * PASSES * K_PASS * COLS
 
@@ -227,6 +229,9 @@ def tile_ctgrucell_kernel(
         def bias_of(gate, j):
             return bias[:, gate * COL_TILES + j : gate * COL_TILES + j + 1]
 
+        def tiles_of(run):
+            return range(run * RUN, (run + 1) * RUN)
+
         rh_sorted = keep.tile([P, B_TILES, PACK, P], BF16)
         rh = {}
 
@@ -234,7 +239,7 @@ def tile_ctgrucell_kernel(
             acc = gate_tile(R, j, H_SUM)
             r = work.tile([P, BATCH], F32, tag="gate")
             nc.scalar.activation(out=r[:], in_=acc[:], func=ACT.Sigmoid, bias=bias_of(R, j), scale=1.0)
-            rh[j] = work.tile([P, BATCH], F32, name="rh", tag="lagged", bufs=LAG + 2)
+            rh[j] = work.tile([P, BATCH], F32, name="rh", tag="lagged", bufs=(LAG + 1) * RUN)
             nc.vector.tensor_mul(out=rh[j][:], in0=r[:], in1=h_turned[:, j, :])
 
         def sum_rh(j):
@@ -250,14 +255,17 @@ def tile_ctgrucell_kernel(
                     op=ALU.add,
                 )
 
-        for j in range(COL_TILES):
-            reset_gate(j)
-            if j >= LAG:
-                sum_rh(j - LAG)
+        for run in range(RUNS):
+            for j in tiles_of(run):
+                reset_gate(j)
+            if run >= LAG:
+                for j in tiles_of(run - LAG):
+                    sum_rh(j)
 
         z = [keep.tile([P, BATCH], F32, name="z%d" % j) for j in range(COL_TILES)]
         minus_kept = [keep.tile([P, BATCH], F32, name="minus_kept%d" % j) for j in range(COL_TILES)]
-        for j in range(COL_TILES):
+
+        def update_gate(j):
             acc = gate_tile(Z, j, H_SUM)
             nc.scalar.activation(out=z[j][:], in_=acc[:], func=ACT.Sigmoid, bias=bias_of(Z, j), scale=1.0)
             nc.vector.scalar_tensor_tensor(
@@ -268,9 +276,14 @@ def tile_ctgrucell_kernel(
                 op0=ALU.subtract,
                 op1=ALU.mult,
             )
-            if j < LAG:
-                sum_rh(COL_TILES - LAG + j)
-            if j == RH_READY:
+
+        for run in range(RUNS):
+            for j in tiles_of(run):
+                update_gate(j)
+            if run < LAG:
+                for j in tiles_of(RUNS - LAG + run):
+                    sum_rh(j)
+            if run == RH_READY:
                 rh_grouped = work.tile([P, BATCH, PACK], BF16, tag="grouped", bufs=2, align_bytes=64)
                 for i in range(B_TILES):
                     group_sorted(rh_sorted, rh_grouped, i, either_engine(i))
@@ -285,7 +298,7 @@ def tile_ctgrucell_kernel(
             acc = gate_tile(H, j, R_H)
             h_hat = work.tile([P, BATCH], F32, tag="gate")
             nc.scalar.activation(out=h_hat[:], in_=acc[:], func=ACT.Tanh, bias=bias_of(H, j), scale=1.0)
-            minus_fresh[j] = work.tile([P, BATCH], F32, name="minus_fresh", tag="lagged", bufs=LAG + 2)
+            minus_fresh[j] = work.tile([P, BATCH], F32, name="minus_fresh", tag="lagged", bufs=(LAG + 1) * RUN)
             nc.vector.scalar_tensor_tensor(
                 out=minus_fresh[j][:],
                 in0=z[j][:],
@@ -328,9 +341,10 @@ def tile_ctgrucell_kernel(
                     in_=output_out[group][:],
                 )
 
-        for j in range(COL_TILES):
-            candidate(j)
-            if j >= LAG:
-                send_back(j - LAG)
-        for j in range(COL_TILES - LAG, COL_TILES):
-            send_back(j)
+        for run in range(RUNS + LAG):
+            if run < RUNS:
+                for j in tiles_of(run):
+                    candidate(j)
+            if run >= LAG:
+                for j in tiles_of(run - LAG):
+                    send_back(j)

@@ -161,13 +161,13 @@ def tile_ctgrucell_kernel(
 
         hsum_sorted = keep.tile([P, B_TILES, PACK, P], BF16)
         for i in range(B_TILES):
-            with nc.allow_low_precision(reason="h_sum is rounded once to bfloat16, as the task says"):
-                nc.vector.tensor_reduce(
-                    out=hsum_sorted[:, i, :, :],
-                    in_=h_nat[i][:].rearrange("b (p t m) -> b t p m", t=PACK, m=SCALES),
-                    axis=AXIS.X,
-                    op=ALU.add,
-                )
+            by_scale = h_nat[i][:].rearrange("b (n m) -> b n m", m=SCALES)
+            halves = work.tile([P, UNITS, 2], F32, tag="halves", bufs=2)
+            nc.vector.tensor_add(out=halves[:], in0=by_scale[:, :, 0:2], in1=by_scale[:, :, 2:4])
+            sorted_halves = halves[:].rearrange("b (p t) e -> b t p e", t=PACK)
+            nc.vector.tensor_add(
+                out=hsum_sorted[:, i, :, :], in0=sorted_halves[:, :, :, 0], in1=sorted_halves[:, :, :, 1]
+            )
 
         h_turned = keep.tile([P, COL_TILES, BATCH], BF16)
 
@@ -232,57 +232,64 @@ def tile_ctgrucell_kernel(
         def tiles_of(run):
             return range(run * RUN, (run + 1) * RUN)
 
+        def h_turned_of(run):
+            return h_turned[:, run * RUN : (run + 1) * RUN, :]
+
         rh_sorted = keep.tile([P, B_TILES, PACK, P], BF16)
         rh = {}
 
-        def reset_gate(j):
-            acc = gate_tile(R, j, H_SUM)
-            r = work.tile([P, BATCH], F32, tag="gate")
-            nc.scalar.activation(out=r[:], in_=acc[:], func=ACT.Sigmoid, bias=bias_of(R, j), scale=1.0)
-            rh[j] = work.tile([P, BATCH], F32, name="rh", tag="lagged", bufs=(LAG + 1) * RUN)
-            nc.vector.tensor_mul(out=rh[j][:], in0=r[:], in1=h_turned[:, j, :])
-
-        def sum_rh(j):
-            back = psum_turn.tile([P, B_TILES, P], F32, tag="turn")
-            for i in range(B_TILES):
-                nc.tensor.transpose(back[:, i, :], rh[j][:, i * P : (i + 1) * P], ident_f32[:])
-            units = TILE_UNITS // PACK
-            with nc.allow_low_precision(reason="r_h is rounded once to bfloat16, as the task says"):
-                nc.vector.tensor_reduce(
-                    out=rh_sorted[:, :, :, j * units : (j + 1) * units],
-                    in_=back[:].rearrange("b i (q t m) -> b i t q m", t=PACK, m=SCALES),
-                    axis=AXIS.X,
-                    op=ALU.add,
+        def reset_gates(run):
+            r = work.tile([P, RUN, BATCH], F32, tag="gate")
+            for k, j in enumerate(tiles_of(run)):
+                acc = gate_tile(R, j, H_SUM)
+                nc.scalar.activation(
+                    out=r[:, k, :], in_=acc[:], func=ACT.Sigmoid, bias=bias_of(R, j), scale=1.0
                 )
+            rh[run] = work.tile([P, RUN, BATCH], F32, name="rh", tag="lagged", bufs=LAG + 1)
+            multiplier = nc.gpsimd if run % 2 else nc.vector
+            multiplier.tensor_tensor(out=rh[run][:], in0=r[:], in1=h_turned_of(run), op=ALU.mult)
+
+        def sum_rh(run):
+            for k, j in enumerate(tiles_of(run)):
+                back = psum_turn.tile([P, B_TILES, P], F32, tag="turn")
+                for i in range(B_TILES):
+                    nc.tensor.transpose(back[:, i, :], rh[run][:, k, i * P : (i + 1) * P], ident_f32[:])
+                units = TILE_UNITS // PACK
+                with nc.allow_low_precision(reason="r_h is rounded once to bfloat16, as the task says"):
+                    nc.vector.tensor_reduce(
+                        out=rh_sorted[:, :, :, j * units : (j + 1) * units],
+                        in_=back[:].rearrange("b i (q t m) -> b i t q m", t=PACK, m=SCALES),
+                        axis=AXIS.X,
+                        op=ALU.add,
+                    )
 
         for run in range(RUNS):
-            for j in tiles_of(run):
-                reset_gate(j)
+            reset_gates(run)
             if run >= LAG:
-                for j in tiles_of(run - LAG):
-                    sum_rh(j)
+                sum_rh(run - LAG)
 
-        z = [keep.tile([P, BATCH], F32, name="z%d" % j) for j in range(COL_TILES)]
-        minus_kept = [keep.tile([P, BATCH], F32, name="minus_kept%d" % j) for j in range(COL_TILES)]
+        z = [keep.tile([P, RUN, BATCH], F32, name="z%d" % run) for run in range(RUNS)]
+        minus_kept = [keep.tile([P, RUN, BATCH], F32, name="minus_kept%d" % run) for run in range(RUNS)]
 
-        def update_gate(j):
-            acc = gate_tile(Z, j, H_SUM)
-            nc.scalar.activation(out=z[j][:], in_=acc[:], func=ACT.Sigmoid, bias=bias_of(Z, j), scale=1.0)
+        def update_gates(run):
+            for k, j in enumerate(tiles_of(run)):
+                acc = gate_tile(Z, j, H_SUM)
+                nc.scalar.activation(
+                    out=z[run][:, k, :], in_=acc[:], func=ACT.Sigmoid, bias=bias_of(Z, j), scale=1.0
+                )
             nc.vector.scalar_tensor_tensor(
-                out=minus_kept[j][:],
-                in0=z[j][:],
+                out=minus_kept[run][:],
+                in0=z[run][:],
                 scalar=1.0,
-                in1=h_turned[:, j, :],
+                in1=h_turned_of(run),
                 op0=ALU.subtract,
                 op1=ALU.mult,
             )
 
         for run in range(RUNS):
-            for j in tiles_of(run):
-                update_gate(j)
+            update_gates(run)
             if run < LAG:
-                for j in tiles_of(RUNS - LAG + run):
-                    sum_rh(j)
+                sum_rh(RUNS - LAG + run)
             if run == RH_READY:
                 rh_grouped = work.tile([P, BATCH, PACK], BF16, tag="grouped", bufs=2, align_bytes=64)
                 for i in range(B_TILES):
@@ -292,59 +299,53 @@ def tile_ctgrucell_kernel(
         new_state = out_1.rearrange("(i b) c -> b i c", b=P)
         output = out_0.rearrange("(i b) n -> b i n", b=P)
         minus_fresh = {}
-        output_out = {}
 
-        def candidate(j):
-            acc = gate_tile(H, j, R_H)
-            h_hat = work.tile([P, BATCH], F32, tag="gate")
-            nc.scalar.activation(out=h_hat[:], in_=acc[:], func=ACT.Tanh, bias=bias_of(H, j), scale=1.0)
-            minus_fresh[j] = work.tile([P, BATCH], F32, name="minus_fresh", tag="lagged", bufs=(LAG + 1) * RUN)
+        def candidates(run):
+            h_hat = work.tile([P, RUN, BATCH], F32, tag="gate")
+            for k, j in enumerate(tiles_of(run)):
+                acc = gate_tile(H, j, R_H)
+                nc.scalar.activation(
+                    out=h_hat[:, k, :], in_=acc[:], func=ACT.Tanh, bias=bias_of(H, j), scale=1.0
+                )
+            minus_fresh[run] = work.tile([P, RUN, BATCH], F32, name="minus_fresh", tag="lagged", bufs=LAG + 1)
             nc.vector.scalar_tensor_tensor(
-                out=minus_fresh[j][:],
-                in0=z[j][:],
+                out=minus_fresh[run][:],
+                in0=z[run][:],
                 scalar=minus_alpha[:, 0:1],
                 in1=h_hat[:],
                 op0=ALU.mult,
                 op1=ALU.mult,
             )
 
-        def send_back(j):
-            back = psum_turn.tile([P, B_TILES, P], F32, tag="turn")
-            for i in range(B_TILES):
-                rows = slice(i * P, (i + 1) * P)
-                nc.tensor.matmul(
-                    out=back[:, i, :], lhsT=minus_kept[j][:, rows], rhs=ident_f32[:],
-                    is_transpose=True, start=True, stop=False,
-                )
-                nc.tensor.matmul(
-                    out=back[:, i, :], lhsT=minus_fresh[j][:, rows], rhs=ident_f32[:],
-                    is_transpose=True, start=False, stop=True,
-                )
-            state_out = work.tile([P, B_TILES, P], F32, tag="state_out")
-            nc.scalar.mul(out=state_out[:], in_=back[:], mul=-1.0)
-            nc.sync.dma_start(out=new_state[:, :, j * P : (j + 1) * P], in_=state_out[:])
-            group = j // GROUP
-            if j % GROUP == 0:
-                output_out[group] = work.tile(
-                    [P, B_TILES, GROUP * TILE_UNITS], F32, name="output_out", tag="output_out", bufs=2
-                )
-            at = (j % GROUP) * TILE_UNITS
+        def send_back(run):
+            state_out = work.tile([P, B_TILES, RUN * P], F32, tag="state_out")
+            for k in range(RUN):
+                back = psum_turn.tile([P, B_TILES, P], F32, tag="turn")
+                for i in range(B_TILES):
+                    rows = slice(i * P, (i + 1) * P)
+                    nc.tensor.matmul(
+                        out=back[:, i, :], lhsT=minus_kept[run][:, k, rows], rhs=ident_f32[:],
+                        is_transpose=True, start=True, stop=False,
+                    )
+                    nc.tensor.matmul(
+                        out=back[:, i, :], lhsT=minus_fresh[run][:, k, rows], rhs=ident_f32[:],
+                        is_transpose=True, start=False, stop=True,
+                    )
+                nc.scalar.mul(out=state_out[:, :, k * P : (k + 1) * P], in_=back[:], mul=-1.0)
+            nc.sync.dma_start(out=new_state[:, :, run * RUN * P : (run + 1) * RUN * P], in_=state_out[:])
+            output_out = work.tile([P, B_TILES, RUN * TILE_UNITS], F32, tag="output_out")
             nc.vector.tensor_reduce(
-                out=output_out[group][:, :, at : at + TILE_UNITS],
+                out=output_out[:],
                 in_=state_out[:].rearrange("b i (n m) -> b i n m", m=SCALES),
                 axis=AXIS.X,
                 op=ALU.add,
             )
-            if j % GROUP == GROUP - 1:
-                nc.sync.dma_start(
-                    out=output[:, :, group * GROUP * TILE_UNITS : (group + 1) * GROUP * TILE_UNITS],
-                    in_=output_out[group][:],
-                )
+            nc.sync.dma_start(
+                out=output[:, :, run * RUN * TILE_UNITS : (run + 1) * RUN * TILE_UNITS], in_=output_out[:]
+            )
 
         for run in range(RUNS + LAG):
             if run < RUNS:
-                for j in tiles_of(run):
-                    candidate(j)
+                candidates(run)
             if run >= LAG:
-                for j in tiles_of(run - LAG):
-                    send_back(j)
+                send_back(run - LAG)

@@ -21,6 +21,7 @@ SCALES = 4
 COLS = UNITS * SCALES
 PACK = 4
 K_PASS = P * PACK
+PLANE_ROWS = 4
 PASSES = 2
 B_TILES = BATCH // P
 COL_TILES = COLS // P
@@ -66,8 +67,9 @@ def tile_ctgrucell_kernel(
         psum_turn = stack.enter_context(tc.psum_pool(name="psum_turn", bufs=4))
         stack.enter_context(tc.manual_schedule())
 
-        planes = keep.tile([P, 2, COLS], U8, align_bytes=64)
-        nc.vector.memset(planes[:].bitcast(I32), 0)
+        planes = keep.tile([P, 3, COLS], U8, align_bytes=64)
+        for gate in (R, Z, H):
+            nc.vector.memset(planes[:, gate, :].bitcast(I32), 0)
         bias_rows = const.tile([P, P], BF16)
         nc.vector.memset(bias_rows[:], 0.0)
         ones = const.tile([P, TILE_UNITS, SCALES], F32)
@@ -87,14 +89,14 @@ def tile_ctgrucell_kernel(
                 nc.sync.dma_start(out=x_nat[:], in_=inputs.rearrange("(i b) k -> b i k", b=P))
             nc.sync.dma_start(out=h_nat[i][:], in_=state[i * P : (i + 1) * P, :])
 
-        def plane_start(gate, g):
-            return 8 * (gate % 2) + 4 * g
+        def plane_start(g):
+            return PLANE_ROWS * g
 
         def load_scales(gate, scales):
             for quadrant in range(4):
-                first = 32 * quadrant + plane_start(gate, 0)
+                first = 32 * quadrant + plane_start(0)
                 nc.sync.dma_start(
-                    out=planes[first : first + 4 * PASSES, gate // 2, :].bitcast(I32),
+                    out=planes[first : first + PLANE_ROWS * PASSES, gate, :].bitcast(I32),
                     in_=scales[:, 4 * quadrant : 4 * quadrant + 4, :].bitcast(I32),
                 )
 
@@ -218,7 +220,7 @@ def tile_ctgrucell_kernel(
                 nc.tensor.matmul_mx(
                     out=acc[:],
                     lhsT=part[:, g, cols].bitcast(FP8X4),
-                    lhsT_scale=planes[plane_start(gate, g) : P, gate // 2, j * P : (j + 1) * P],
+                    lhsT_scale=planes[plane_start(g) : P, gate, j * P : (j + 1) * P],
                     rhs=act_codes[:, slot, :].bitcast(FP8X4),
                     rhs_scale=act_scales[:, slot, :],
                     start=(g == 0),

@@ -140,7 +140,10 @@ def tile_ctgrucell_kernel(
         def group_rows(planes, grouped_rows, ident, copy_out):
             turned = psum_turn.tile([P, len(planes), P], ident.dtype, tag="turn")
             for k in range(len(planes)):
-                nc.tensor.transpose(turned[:, k, :], planes[k], ident)
+                if ident.dtype == BF16:
+                    nc.tensor.matmul(out=turned[:, k, :], lhsT=planes[k], rhs=ident, start=True, stop=True)
+                else:
+                    nc.tensor.transpose(turned[:, k, :], planes[k], ident)
             copy_out(out=grouped_rows, in_=turned[:].rearrange("p k b -> p b k"))
 
         def group_sorted(sorted_nat, grouped, i, copy_out):
@@ -178,7 +181,13 @@ def tile_ctgrucell_kernel(
                 turned = psum_turn.tile([P, GROUP, P], BF16, tag="turn")
                 for jj in range(GROUP):
                     j = quarter * GROUP + jj
-                    nc.tensor.transpose(turned[:, jj, :], h_nat[i][:, j * P : (j + 1) * P], ident_bf[:])
+                    nc.tensor.matmul(
+                        out=turned[:, jj, :],
+                        lhsT=h_nat[i][:, j * P : (j + 1) * P],
+                        rhs=ident_bf[:],
+                        start=True,
+                        stop=True,
+                    )
                 copy_out(
                     out=h_turned[:, quarter * GROUP : (quarter + 1) * GROUP, i * P : (i + 1) * P],
                     in_=turned[:],

@@ -31,7 +31,7 @@ HALF_TILES = COL_TILES // 2
 RUN = 2
 RUNS = COL_TILES // RUN
 LAG = 2
-RH_READY = LAG
+RH_READY = LAG + 1
 
 FLOPS = 3 * 2 * BATCH * PASSES * K_PASS * COLS
 
@@ -310,6 +310,7 @@ def tile_ctgrucell_kernel(
         new_state = out_1.rearrange("(i b) c -> b i c", b=P)
         output = out_0.rearrange("(i b) n -> b i n", b=P)
         minus_fresh = {}
+        out_halves = {}
 
         def candidates(run):
             h_hat = work.tile([P, RUN, BATCH], F32, tag="gate")
@@ -329,7 +330,8 @@ def tile_ctgrucell_kernel(
             )
 
         def send_back(run):
-            state_out = work.tile([P, B_TILES, RUN * P], F32, tag="state_out")
+            state_out = work.tile([P, B_TILES, RUN * P], F32, tag="state_out", bufs=4)
+            out_halves[run] = work.tile([P, B_TILES, RUN * TILE_UNITS, 2], F32, name="out_halves", tag="out_halves")
             for k in range(RUN):
                 back = psum_turn.tile([P, B_TILES, P], F32, tag="turn")
                 for i in range(B_TILES):
@@ -343,20 +345,37 @@ def tile_ctgrucell_kernel(
                         is_transpose=True, start=False, stop=True,
                     )
                 nc.scalar.mul(out=state_out[:, :, k * P : (k + 1) * P], in_=back[:], mul=-1.0)
-            nc.sync.dma_start(out=new_state[:, :, run * RUN * P : (run + 1) * RUN * P], in_=state_out[:])
-            output_out = work.tile([P, B_TILES, RUN * TILE_UNITS], F32, tag="output_out")
-            nc.vector.tensor_reduce(
-                out=output_out[:],
-                in_=state_out[:].rearrange("b i (n m) -> b i n m", m=SCALES),
-                axis=AXIS.X,
-                op=ALU.add,
+                if run == RUNS - 1:
+                    finish(run, state_out, k, 1)
+            if run < RUNS - 1:
+                finish(run, state_out, 0, RUN)
+
+        def finish(run, state_out, k, tiles):
+            cols = slice(k * P, (k + tiles) * P)
+            nc.sync.dma_start(
+                out=new_state[:, :, (run * RUN + k) * P : (run * RUN + k + tiles) * P],
+                in_=state_out[:, :, cols],
+            )
+            by_scale = state_out[:, :, cols].rearrange("b i (n m) -> b i n m", m=SCALES)
+            nc.vector.tensor_add(
+                out=out_halves[run][:, :, k * TILE_UNITS : (k + tiles) * TILE_UNITS, :],
+                in0=by_scale[:, :, :, 0:2],
+                in1=by_scale[:, :, :, 2:4],
+            )
+
+        def sum_output(run):
+            output_out = work.tile([P, B_TILES, RUN * TILE_UNITS], F32, tag="output_out", bufs=4)
+            nc.vector.tensor_add(
+                out=output_out[:], in0=out_halves[run][:, :, :, 0], in1=out_halves[run][:, :, :, 1]
             )
             nc.sync.dma_start(
                 out=output[:, :, run * RUN * TILE_UNITS : (run + 1) * RUN * TILE_UNITS], in_=output_out[:]
             )
 
-        for run in range(RUNS + LAG):
+        for run in range(RUNS + LAG + 1):
             if run < RUNS:
                 candidates(run)
-            if run >= LAG:
+            if LAG <= run < RUNS + LAG:
                 send_back(run - LAG)
+            if run > LAG:
+                sum_output(run - LAG - 1)

@@ -256,7 +256,7 @@ def tile_ctgrucell_kernel(
                 nc.scalar.activation(
                     out=r[:, k, :], in_=acc[:], func=ACT.Sigmoid, bias=bias_of(R, j), scale=1.0
                 )
-            rh[run] = work.tile([P, RUN, BATCH], F32, name="rh", tag="lagged", bufs=LAG + 1)
+            rh[run] = work.tile([P, RUN, BATCH], F32, name="rh", tag="lagged", bufs=LAG + 2)
             multiplier = nc.gpsimd if run % 2 else nc.vector
             multiplier.tensor_tensor(out=rh[run][:], in0=r[:], in1=h_turned_of(run), op=ALU.mult)
 
@@ -274,10 +274,12 @@ def tile_ctgrucell_kernel(
                         op=ALU.add,
                     )
 
-        for run in range(RUNS):
+        for run in range(0, RUNS, 2):
             reset_gates(run)
+            reset_gates(run + 1)
             if run >= LAG:
                 sum_rh(run - LAG)
+                sum_rh(run - LAG + 1)
 
         z = [keep.tile([P, RUN, BATCH], F32, name="z%d" % run) for run in range(RUNS)]
         minus_kept = [keep.tile([P, RUN, BATCH], F32, name="minus_kept%d" % run) for run in range(RUNS)]
@@ -319,7 +321,7 @@ def tile_ctgrucell_kernel(
                 nc.scalar.activation(
                     out=h_hat[:, k, :], in_=acc[:], func=ACT.Tanh, bias=bias_of(H, j), scale=1.0
                 )
-            minus_fresh[run] = work.tile([P, RUN, BATCH], F32, name="minus_fresh", tag="lagged", bufs=LAG + 1)
+            minus_fresh[run] = work.tile([P, RUN, BATCH], F32, name="minus_fresh", tag="lagged", bufs=LAG + 2)
             nc.vector.scalar_tensor_tensor(
                 out=minus_fresh[run][:],
                 in0=z[run][:],
@@ -330,7 +332,7 @@ def tile_ctgrucell_kernel(
             )
 
         def send_back(run):
-            state_out = work.tile([P, B_TILES, RUN * P], F32, tag="state_out", bufs=4)
+            state_out = work.tile([P, B_TILES, RUN * P], F32, tag="state_out")
             out_halves[run] = work.tile([P, B_TILES, RUN * TILE_UNITS, 2], F32, name="out_halves", tag="out_halves")
             for k in range(RUN):
                 back = psum_turn.tile([P, B_TILES, P], F32, tag="turn")
@@ -372,10 +374,12 @@ def tile_ctgrucell_kernel(
                 out=output[:, :, run * RUN * TILE_UNITS : (run + 1) * RUN * TILE_UNITS], in_=output_out[:]
             )
 
-        for run in range(RUNS + LAG + 1):
+        for run in range(0, RUNS + LAG, 2):
             if run < RUNS:
                 candidates(run)
-            if LAG <= run < RUNS + LAG:
+                candidates(run + 1)
+            if run >= LAG:
                 send_back(run - LAG)
-            if run > LAG:
-                sum_output(run - LAG - 1)
+                send_back(run - LAG + 1)
+                sum_output(run - LAG)
+                sum_output(run - LAG + 1)

@@ -42,6 +42,11 @@ R, Z, H = 0, 1, 2
 X, H_SUM, R_H = 0, 1, 2
 
 
+def pieces_of(length, pieces):
+    step = length // pieces
+    return [slice(k * step, (k + 1) * step) for k in range(pieces)]
+
+
 def tile_ctgrucell_kernel(
     tc,
     inputs,
@@ -83,11 +88,14 @@ def tile_ctgrucell_kernel(
         nc.scalar.activation(out=table_warmer[:], in_=ones[:, 0, 0:1], func=ACT.Sigmoid)
 
         x_nat = keep.tile([P, B_TILES, K_PASS], BF16)
-        h_nat = [keep.tile([P, COLS], BF16, name="h_nat%d" % i) for i in range(B_TILES)]
+        h_all = keep.tile([P, B_TILES, COLS], BF16)
+        h_nat = [h_all[:, i, :] for i in range(B_TILES)]
         for i in range(B_TILES):
             if i == B_TILES // 2:
                 nc.sync.dma_start(out=x_nat[:], in_=inputs.rearrange("(i b) k -> b i k", b=P))
-            nc.sync.dma_start(out=h_nat[i][:], in_=state[i * P : (i + 1) * P, :])
+            pieces = 2 if i == 0 else 1
+            for cols in pieces_of(COLS, pieces):
+                nc.sync.dma_start(out=h_nat[i][:, cols], in_=state[i * P : (i + 1) * P, cols])
 
         def plane_start(g):
             return PLANE_ROWS * g
@@ -157,18 +165,21 @@ def tile_ctgrucell_kernel(
         def either_engine(i):
             return nc.vector.tensor_copy if i % 2 else nc.scalar.copy
 
-        def quantise(grouped, slot):
+        def quantise(grouped, slot, rows=slice(0, BATCH)):
             nc.vector.quantize_mx(
-                out=act_codes[:, slot, :].bitcast(FP8X4),
-                scales=act_scales[:, slot, :],
-                in_=grouped[:].rearrange("p b t -> p (b t)"),
+                out=act_codes[:, slot, rows].bitcast(FP8X4),
+                scales=act_scales[:, slot, rows],
+                in_=grouped[:, rows, :].rearrange("p b t -> p (b t)"),
             )
 
         hsum_sorted = keep.tile([P, B_TILES, PACK, P], BF16)
         for i in range(B_TILES):
-            by_scale = h_nat[i][:].rearrange("b (n m) -> b n m", m=SCALES)
+            by_scale = h_nat[i].rearrange("b (n m) -> b n m", m=SCALES)
             halves = work.tile([P, UNITS, 2], F32, tag="halves", bufs=2)
-            nc.vector.tensor_add(out=halves[:], in0=by_scale[:, :, 0:2], in1=by_scale[:, :, 2:4])
+            for units in pieces_of(UNITS, 2 if i == 0 else 1):
+                nc.vector.tensor_add(
+                    out=halves[:, units, :], in0=by_scale[:, units, 0:2], in1=by_scale[:, units, 2:4]
+                )
             sorted_halves = halves[:].rearrange("b (p t) e -> b t p e", t=PACK)
             nc.vector.tensor_add(
                 out=hsum_sorted[:, i, :, :], in0=sorted_halves[:, :, :, 0], in1=sorted_halves[:, :, :, 1]
@@ -218,7 +229,8 @@ def tile_ctgrucell_kernel(
         hsum_grouped = work.tile([P, BATCH, PACK], BF16, tag="grouped", bufs=2, align_bytes=64)
         for i in range(B_TILES):
             group_sorted(hsum_sorted, hsum_grouped, i, nc.scalar.copy)
-        quantise(hsum_grouped, H_SUM)
+            if i:
+                quantise(hsum_grouped, H_SUM, slice((i if i > 1 else 0) * P, (i + 1) * P))
         turn_state(3, nc.vector.tensor_copy)
 
         def gate_tile(gate, j, state_slot):
@@ -257,7 +269,7 @@ def tile_ctgrucell_kernel(
                     out=r[:, k, :], in_=acc[:], func=ACT.Sigmoid, bias=bias_of(R, j), scale=1.0
                 )
             rh[run] = work.tile([P, RUN, BATCH], F32, name="rh", tag="lagged", bufs=LAG + 2)
-            multiplier = nc.gpsimd if run % 2 else nc.vector
+            multiplier = nc.gpsimd if run % 2 and run > 1 else nc.vector
             multiplier.tensor_tensor(out=rh[run][:], in0=r[:], in1=h_turned_of(run), op=ALU.mult)
 
         def sum_rh(run):
@@ -284,12 +296,17 @@ def tile_ctgrucell_kernel(
         z = [keep.tile([P, RUN, BATCH], F32, name="z%d" % run) for run in range(RUNS)]
         minus_kept = [keep.tile([P, RUN, BATCH], F32, name="minus_kept%d" % run) for run in range(RUNS)]
 
+        def adds_on_vector(run):
+            return run == 1
+
         def update_gates(run):
             for k, j in enumerate(tiles_of(run)):
                 acc = gate_tile(Z, j, H_SUM)
                 nc.scalar.activation(
                     out=z[run][:, k, :], in_=acc[:], func=ACT.Sigmoid, bias=bias_of(Z, j), scale=1.0
                 )
+            if adds_on_vector(run):
+                return
             nc.vector.scalar_tensor_tensor(
                 out=minus_kept[run][:],
                 in0=z[run][:],
@@ -322,14 +339,29 @@ def tile_ctgrucell_kernel(
                     out=h_hat[:, k, :], in_=acc[:], func=ACT.Tanh, bias=bias_of(H, j), scale=1.0
                 )
             minus_fresh[run] = work.tile([P, RUN, BATCH], F32, name="minus_fresh", tag="lagged", bufs=LAG + 2)
-            nc.vector.scalar_tensor_tensor(
-                out=minus_fresh[run][:],
-                in0=z[run][:],
-                scalar=minus_alpha[:, 0:1],
-                in1=h_hat[:],
-                op0=ALU.mult,
-                op1=ALU.mult,
-            )
+            if adds_on_vector(run):
+                nc.vector.scalar_tensor_tensor(
+                    out=minus_fresh[run][:],
+                    in0=h_hat[:],
+                    scalar=minus_alpha[:, 0:1],
+                    in1=h_turned_of(run),
+                    op0=ALU.mult,
+                    op1=ALU.add,
+                )
+                return
+            for tiles in pieces_of(RUN, RUN if run == RUNS - 1 else 1):
+                nc.vector.scalar_tensor_tensor(
+                    out=minus_fresh[run][:, tiles, :],
+                    in0=z[run][:, tiles, :],
+                    scalar=minus_alpha[:, 0:1],
+                    in1=h_hat[:, tiles, :],
+                    op0=ALU.mult,
+                    op1=ALU.mult,
+                )
+
+        def weigh(run):
+            if adds_on_vector(run):
+                nc.vector.tensor_mul(out=minus_fresh[run][:], in0=z[run][:], in1=minus_fresh[run][:])
 
         def send_back(run):
             state_out = work.tile([P, B_TILES, RUN * P], F32, tag="state_out")
@@ -338,15 +370,20 @@ def tile_ctgrucell_kernel(
                 back = psum_turn.tile([P, B_TILES, P], F32, tag="turn")
                 for i in range(B_TILES):
                     rows = slice(i * P, (i + 1) * P)
-                    nc.tensor.matmul(
-                        out=back[:, i, :], lhsT=minus_kept[run][:, k, rows], rhs=ident_f32[:],
-                        is_transpose=True, start=True, stop=False,
+                    terms = [minus_fresh] if adds_on_vector(run) else [minus_kept, minus_fresh]
+                    for term in terms:
+                        nc.tensor.matmul(
+                            out=back[:, i, :], lhsT=term[run][:, k, rows], rhs=ident_f32[:],
+                            is_transpose=True, start=(term is terms[0]), stop=(term is minus_fresh),
+                        )
+                if adds_on_vector(run):
+                    nc.vector.tensor_sub(
+                        out=state_out[:, :, k * P : (k + 1) * P],
+                        in0=h_all[:, :, (run * RUN + k) * P : (run * RUN + k + 1) * P],
+                        in1=back[:],
                     )
-                    nc.tensor.matmul(
-                        out=back[:, i, :], lhsT=minus_fresh[run][:, k, rows], rhs=ident_f32[:],
-                        is_transpose=True, start=False, stop=True,
-                    )
-                nc.scalar.mul(out=state_out[:, :, k * P : (k + 1) * P], in_=back[:], mul=-1.0)
+                else:
+                    nc.scalar.mul(out=state_out[:, :, k * P : (k + 1) * P], in_=back[:], mul=-1.0)
                 if run == RUNS - 1:
                     finish(run, state_out, k, 1)
             if run < RUNS - 1:
@@ -380,6 +417,10 @@ def tile_ctgrucell_kernel(
                 candidates(run + 1)
             if run >= LAG:
                 send_back(run - LAG)
+            if run < RUNS:
+                weigh(run)
+                weigh(run + 1)
+            if run >= LAG:
                 send_back(run - LAG + 1)
                 sum_output(run - LAG)
                 sum_output(run - LAG + 1)

@@ -73,17 +73,20 @@ def tile_ctgrucell_kernel(
         stack.enter_context(tc.manual_schedule())
 
         planes = keep.tile([P, 3, COLS], U8, align_bytes=64)
-        for gate in (R, Z, H):
-            nc.vector.memset(planes[:, gate, :].bitcast(I32), 0)
+        nc.vector.memset(planes[:, R, :].bitcast(I32), 0)
         bias_rows = const.tile([P, P], BF16)
         nc.vector.memset(bias_rows[:], 0.0)
         ones = const.tile([P, TILE_UNITS, SCALES], F32)
         nc.vector.memset(ones[:], 1.0)
         alpha_rows = const.tile([P, TILE_UNITS, SCALES], F32)
-        for m in range(SCALES):
-            nc.vector.tensor_scalar_mul(out=alpha_rows[:, :, m], in0=ones[:, :, m], scalar1=-ALPHA[m])
         ident_f32 = const.tile([P, P], F32)
         make_identity(nc, ident_f32[:])
+        ident_bf = const.tile([P, P], BF16)
+        nc.vector.tensor_copy(out=ident_bf[:], in_=ident_f32[:])
+        for gate in (Z, H):
+            nc.vector.memset(planes[:, gate, :].bitcast(I32), 0)
+        for m in range(SCALES):
+            nc.vector.tensor_scalar_mul(out=alpha_rows[:, :, m], in0=ones[:, :, m], scalar1=-ALPHA[m])
         table_warmer = const.tile([P, 1], F32)
         nc.scalar.activation(out=table_warmer[:], in_=ones[:, 0, 0:1], func=ACT.Sigmoid)
 
@@ -135,13 +138,6 @@ def tile_ctgrucell_kernel(
                 in_=b.rearrange("(j c) -> j c", c=P),
             )
 
-        ident_bf = const.tile([P, P], BF16)
-        nc.vector.tensor_copy(out=ident_bf[:], in_=ident_f32[:])
-        alpha_turned = psum_turn.tile([P, P], F32, tag="turn")
-        nc.tensor.transpose(alpha_turned[:], alpha_rows[:].rearrange("p n m -> p (n m)"), ident_f32[:])
-        minus_alpha = const.tile([P, 1], F32)
-        nc.vector.tensor_copy(out=minus_alpha[:], in_=alpha_turned[:, 0:1])
-
         act_codes = keep.tile([P, 3, BATCH], U32, align_bytes=64)
         act_scales = keep.tile([P, 3, BATCH], U8, align_bytes=64)
 
@@ -172,7 +168,7 @@ def tile_ctgrucell_kernel(
                 in_=grouped[:, rows, :].rearrange("p b t -> p (b t)"),
             )
 
-        hsum_sorted = keep.tile([P, B_TILES, PACK, P], BF16)
+        hsum_sorted = keep.tile([P, B_TILES, 2, P, 2], BF16)
         for i in range(B_TILES):
             by_scale = h_nat[i].rearrange("b (n m) -> b n m", m=SCALES)
             halves = work.tile([P, UNITS, 2], F32, tag="halves", bufs=2)
@@ -180,9 +176,9 @@ def tile_ctgrucell_kernel(
                 nc.vector.tensor_add(
                     out=halves[:, units, :], in0=by_scale[:, units, 0:2], in1=by_scale[:, units, 2:4]
                 )
-            sorted_halves = halves[:].rearrange("b (p t) e -> b t p e", t=PACK)
+            sorted_halves = halves[:].rearrange("b (p u v) e -> b u p v e", u=2, v=2)
             nc.vector.tensor_add(
-                out=hsum_sorted[:, i, :, :], in0=sorted_halves[:, :, :, 0], in1=sorted_halves[:, :, :, 1]
+                out=hsum_sorted[:, i, :, :, :], in0=sorted_halves[:, :, :, :, 0], in1=sorted_halves[:, :, :, :, 1]
             )
 
         h_turned = keep.tile([P, COL_TILES, BATCH], BF16)
@@ -209,6 +205,10 @@ def tile_ctgrucell_kernel(
         nc.tensor.transpose(bias_turned[:], bias_rows[:], ident_bf[:])
         bias = const.tile([P, P], F32)
         nc.scalar.copy(out=bias[:], in_=bias_turned[:])
+        alpha_turned = psum_turn.tile([P, P], F32, tag="turn")
+        nc.tensor.transpose(alpha_turned[:], alpha_rows[:].rearrange("p n m -> p (n m)"), ident_f32[:])
+        minus_alpha = const.tile([P, 1], F32)
+        nc.scalar.copy(out=minus_alpha[:], in_=alpha_turned[:, 0:1])
         turn_state(1, nc.scalar.copy)
 
         x_grouped = work.tile([P, BATCH, PACK], BF16, tag="grouped", bufs=2, align_bytes=64)
@@ -227,8 +227,17 @@ def tile_ctgrucell_kernel(
         turn_state(2, nc.scalar.copy)
 
         hsum_grouped = work.tile([P, BATCH, PACK], BF16, tag="grouped", bufs=2, align_bytes=64)
+        hsum_grouped_words = (
+            hsum_grouped[:].rearrange("p b t -> p (b t)").bitcast(F32).rearrange("p (b u) -> p b u", u=2)
+        )
         for i in range(B_TILES):
-            group_sorted(hsum_sorted, hsum_grouped, i, nc.scalar.copy)
+            hsum_words = hsum_sorted[:, i, :, :, :].rearrange("b u p v -> b (u p v)").bitcast(F32)
+            group_rows(
+                [hsum_words[:, u * P : (u + 1) * P] for u in range(2)],
+                hsum_grouped_words[:, i * P : (i + 1) * P, :],
+                ident_f32[:],
+                nc.scalar.copy,
+            )
             if i:
                 quantise(hsum_grouped, H_SUM, slice((i if i > 1 else 0) * P, (i + 1) * P))
         turn_state(3, nc.vector.tensor_copy)
@@ -318,8 +327,9 @@ def tile_ctgrucell_kernel(
 
         for run in range(RUNS):
             update_gates(run)
-            if run < LAG:
-                sum_rh(RUNS - LAG + run)
+            if run == LAG - 1:
+                sum_rh(RUNS - LAG)
+                sum_rh(RUNS - 1)
             if run == RH_READY:
                 rh_grouped = work.tile([P, BATCH, PACK], BF16, tag="grouped", bufs=2, align_bytes=64)
                 for i in range(B_TILES):

@@ -182,6 +182,9 @@ def tile_ctgrucell_kernel(
             )
 
         h_turned = keep.tile([P, COL_TILES, BATCH], BF16)
+        h_turned_words = (
+            h_turned[:].rearrange("c j b -> c (j b)").bitcast(F32).rearrange("c (j w) -> c j w", j=COL_TILES)
+        )
 
         def turn_state(i, copy_out):
             for quarter in range(COL_TILES // GROUP):
@@ -195,9 +198,10 @@ def tile_ctgrucell_kernel(
                         start=True,
                         stop=True,
                     )
+                words = slice(i * P // 2, (i + 1) * P // 2)
                 copy_out(
-                    out=h_turned[:, quarter * GROUP : (quarter + 1) * GROUP, i * P : (i + 1) * P],
-                    in_=turned[:],
+                    out=h_turned_words[:, quarter * GROUP : (quarter + 1) * GROUP, words],
+                    in_=turned[:].rearrange("c j b -> c (j b)").bitcast(F32).rearrange("c (j w) -> c j w", j=GROUP),
                 )
 
         turn_state(0, nc.scalar.copy)

import math
from contextlib import ExitStack

import concourse.mybir as mybir
from concourse.masks import make_identity

F32 = mybir.dt.float32
BF16 = mybir.dt.bfloat16
I32 = mybir.dt.int32
U32 = mybir.dt.uint32
U8 = mybir.dt.uint8
FP8X4 = mybir.dt.float8_e4m3fn_x4
ACT = mybir.ActivationFunctionType
ALU = mybir.AluOpType
AXIS = mybir.AxisListType

P = 128
BATCH = 512
UNITS = 512
SCALES = 4
COLS = UNITS * SCALES
PACK = 4
K_PASS = P * PACK
PLANE_ROWS = 4
PASSES = 2
B_TILES = BATCH // P
COL_TILES = COLS // P
TILE_UNITS = P // SCALES
GROUP = 4
HALF_TILES = COL_TILES // 2
RUN = 2
RUNS = COL_TILES // RUN
LAG = 2
RH_READY = LAG + 1

FLOPS = 3 * 2 * BATCH * PASSES * K_PASS * COLS

DECAY = [math.exp(-0.5 * math.log(10.0) * m) for m in range(SCALES)]
ALPHA = [d / sum(DECAY) for d in DECAY]

R, Z, H = 0, 1, 2
X, H_SUM, R_H = 0, 1, 2


def pieces_of(length, pieces):
    step = length // pieces
    return [slice(k * step, (k + 1) * step) for k in range(pieces)]


def tile_ctgrucell_kernel(
    tc,
    inputs,
    state,
    W_z_words,
    W_z_scales,
    b_z,
    W_r_words,
    W_r_scales,
    b_r,
    W_h_words,
    W_h_scales,
    b_h,
    out_0,
    out_1,
):
    nc = tc.nc
    with ExitStack() as stack:
        const = stack.enter_context(tc.tile_pool(name="const", bufs=1))
        keep = stack.enter_context(tc.tile_pool(name="keep", bufs=1))
        work = stack.enter_context(tc.tile_pool(name="work", bufs=3))
        psum_acc = stack.enter_context(tc.psum_pool(name="psum_acc", bufs=4))
        psum_turn = stack.enter_context(tc.psum_pool(name="psum_turn", bufs=4))
        stack.enter_context(tc.manual_schedule())

        planes = keep.tile([P, 3, COLS], U8, align_bytes=64)
        nc.vector.memset(planes[:, R, :].bitcast(I32), 0)
        bias_rows = const.tile([P, P], BF16)
        nc.vector.memset(bias_rows[:], 0.0)
        ones = const.tile([P, TILE_UNITS, SCALES], F32)
        nc.vector.memset(ones[:], 1.0)
        alpha_rows = const.tile([P, TILE_UNITS, SCALES], F32)
        ident_f32 = const.tile([P, P], F32)
        make_identity(nc, ident_f32[:])
        ident_bf = const.tile([P, P], BF16)
        nc.vector.tensor_copy(out=ident_bf[:], in_=ident_f32[:])
        for gate in (Z, H):
            nc.vector.memset(planes[:, gate, :].bitcast(I32), 0)
        for m in range(SCALES):
            nc.vector.tensor_scalar_mul(out=alpha_rows[:, :, m], in0=ones[:, :, m], scalar1=-ALPHA[m])
        table_warmer = const.tile([P, 1], F32)
        nc.scalar.activation(out=table_warmer[:], in_=ones[:, 0, 0:1], func=ACT.Sigmoid)

        x_nat = keep.tile([P, B_TILES, K_PASS], BF16)
        h_all = keep.tile([P, B_TILES, COLS], BF16)
        h_nat = [h_all[:, i, :] for i in range(B_TILES)]
        for i in range(B_TILES):
            if i == B_TILES // 2:
                nc.sync.dma_start(out=x_nat[:], in_=inputs.rearrange("(i b) k -> b i k", b=P))
            pieces = 2 if i == 0 else 1
            for cols in pieces_of(COLS, pieces):
                nc.sync.dma_start(out=h_nat[i][:, cols], in_=state[i * P : (i + 1) * P, cols])

        def plane_start(g):
            return PLANE_ROWS * g

        def load_scales(gate, scales):
            for quadrant in range(4):
                first = 32 * quadrant + plane_start(0)
                nc.sync.dma_start(
                    out=planes[first : first + PLANE_ROWS * PASSES, gate, :].bitcast(I32),
                    in_=scales[:, 4 * quadrant : 4 * quadrant + 4, :].bitcast(I32),
                )

        def load_words(gate, words):
            halves = []
            for half in range(2):
                cols = slice(half * HALF_TILES * P, (half + 1) * HALF_TILES * P)
                part = keep.tile(
                    [P, PASSES, HALF_TILES * P], U32, name="words%d_%d" % (gate, half), align_bytes=64
                )
                nc.sync.dma_start(
                    out=part[:].bitcast(I32),
                    in_=words[:, :, cols, :].rearrange("g p c t -> p g (c t)").bitcast(I32),
                )
                halves.append(part)
            return halves

        w_words = {}
        load_scales(R, W_r_scales)
        w_words[R] = load_words(R, W_r_words)
        load_scales(Z, W_z_scales)
        load_scales(H, W_h_scales)
        w_words[Z] = load_words(Z, W_z_words)
        w_words[H] = load_words(H, W_h_words)
        for gate, b in ((R, b_r), (Z, b_z), (H, b_h)):
            nc.scalar.dma_start(
                out=bias_rows[gate * COL_TILES : (gate + 1) * COL_TILES, :],
                in_=b.rearrange("(j c) -> j c", c=P),
            )

        act_codes = keep.tile([P, 3, BATCH], U32, align_bytes=64)
        act_scales = keep.tile([P, 3, BATCH], U8, align_bytes=64)

        def group_rows(planes, grouped_rows, ident, copy_out):
            turned = psum_turn.tile([P, len(planes), P], ident.dtype, tag="turn")
            for k in range(len(planes)):
                if ident.dtype == BF16:
                    nc.tensor.matmul(out=turned[:, k, :], lhsT=planes[k], rhs=ident, start=True, stop=True)
                else:
                    nc.tensor.transpose(turned[:, k, :], planes[k], ident)
            copy_out(out=grouped_rows, in_=turned[:].rearrange("p k b -> p b k"))

        def group_sorted(sorted_nat, grouped, i, copy_out):
            group_rows(
                [sorted_nat[:, i, t, :] for t in range(PACK)],
                grouped[:, i * P : (i + 1) * P, :],
                ident_bf[:],
                copy_out,
            )

        def either_engine(i):
            return nc.vector.tensor_copy if i % 2 else nc.scalar.copy

        def quantise(grouped, slot, rows=slice(0, BATCH)):
            nc.vector.quantize_mx(
                out=act_codes[:, slot, rows].bitcast(FP8X4),
                scales=act_scales[:, slot, rows],
                in_=grouped[:, rows, :].rearrange("p b t -> p (b t)"),
            )

        hsum_sorted = keep.tile([P, B_TILES, 2, P, 2], BF16)
        for i in range(B_TILES):
            by_scale = h_nat[i].rearrange("b (n m) -> b n m", m=SCALES)
            halves = work.tile([P, UNITS, 2], F32, tag="halves", bufs=2)
            for units in pieces_of(UNITS, 2 if i == 0 else 1):
                nc.vector.tensor_add(
                    out=halves[:, units, :], in0=by_scale[:, units, 0:2], in1=by_scale[:, units, 2:4]
                )
            sorted_halves = halves[:].rearrange("b (p u v) e -> b u p v e", u=2, v=2)
            nc.vector.tensor_add(
                out=hsum_sorted[:, i, :, :, :], in0=sorted_halves[:, :, :, :, 0], in1=sorted_halves[:, :, :, :, 1]
            )

        h_turned = keep.tile([P, COL_TILES, BATCH], BF16)
        h_turned_words = (
            h_turned[:].rearrange("c j b -> c (j b)").bitcast(F32).rearrange("c (j w) -> c j w", j=COL_TILES)
        )

        def turn_state(i, copy_out):
            for quarter in range(COL_TILES // GROUP):
                turned = psum_turn.tile([P, GROUP, P], BF16, tag="turn")
                for jj in range(GROUP):
                    j = quarter * GROUP + jj
                    nc.tensor.matmul(
                        out=turned[:, jj, :],
                        lhsT=h_nat[i][:, j * P : (j + 1) * P],
                        rhs=ident_bf[:],
                        start=True,
                        stop=True,
                    )
                words = slice(i * P // 2, (i + 1) * P // 2)
                copy_out(
                    out=h_turned_words[:, quarter * GROUP : (quarter + 1) * GROUP, words],
                    in_=turned[:].rearrange("c j b -> c (j b)").bitcast(F32).rearrange("c (j w) -> c j w", j=GROUP),
                )

        turn_state(0, nc.scalar.copy)
        bias_turned = psum_turn.tile([P, P], BF16, tag="turn")
        nc.tensor.transpose(bias_turned[:], bias_rows[:], ident_bf[:])
        bias = const.tile([P, P], F32)
        nc.scalar.copy(out=bias[:], in_=bias_turned[:])
        alpha_turned = psum_turn.tile([P, P], F32, tag="turn")
        nc.tensor.transpose(alpha_turned[:], alpha_rows[:].rearrange("p n m -> p (n m)"), ident_f32[:])
        minus_alpha = const.tile([P, 1], F32)
        nc.scalar.copy(out=minus_alpha[:], in_=alpha_turned[:, 0:1])
        turn_state(1, nc.scalar.copy)

        x_grouped = work.tile([P, BATCH, PACK], BF16, tag="grouped", bufs=2, align_bytes=64)
        x_grouped_words = (
            x_grouped[:].rearrange("p b t -> p (b t)").bitcast(F32).rearrange("p (b u) -> p b u", u=2)
        )
        for i in range(B_TILES):
            x_words = x_nat[:, i, :].bitcast(F32)
            group_rows(
                [x_words[:, u : K_PASS // 2 : 2] for u in range(2)],
                x_grouped_words[:, i * P : (i + 1) * P, :],
                ident_f32[:],
                nc.scalar.copy,
            )
        quantise(x_grouped, X)
        turn_state(2, nc.scalar.copy)

        hsum_grouped = work.tile([P, BATCH, PACK], BF16, tag="grouped", bufs=2, align_bytes=64)
        hsum_grouped_words = (
            hsum_grouped[:].rearrange("p b t -> p (b t)").bitcast(F32).rearrange("p (b u) -> p b u", u=2)
        )
        for i in range(B_TILES):
            hsum_words = hsum_sorted[:, i, :, :, :].rearrange("b u p v -> b (u p v)").bitcast(F32)
            group_rows(
                [hsum_words[:, u * P : (u + 1) * P] for u in range(2)],
                hsum_grouped_words[:, i * P : (i + 1) * P, :],
                ident_f32[:],
                nc.scalar.copy,
            )
            if i:
                quantise(hsum_grouped, H_SUM, slice((i if i > 1 else 0) * P, (i + 1) * P))
        turn_state(3, nc.vector.tensor_copy)

        def gate_tile(gate, j, state_slot):
            acc = psum_acc.tile([P, BATCH], F32, tag="acc")
            part = w_words[gate][j // HALF_TILES]
            cols = slice((j % HALF_TILES) * P, (j % HALF_TILES + 1) * P)
            for g, slot in enumerate((X, state_slot)):
                nc.tensor.matmul_mx(
                    out=acc[:],
                    lhsT=part[:, g, cols].bitcast(FP8X4),
                    lhsT_scale=planes[plane_start(g) : P, gate, j * P : (j + 1) * P],
                    rhs=act_codes[:, slot, :].bitcast(FP8X4),
                    rhs_scale=act_scales[:, slot, :],
                    start=(g == 0),
                    stop=(g == PASSES - 1),
                )
            return acc

        def bias_of(gate, j):
            return bias[:, gate * COL_TILES + j : gate * COL_TILES + j + 1]

        def tiles_of(run):
            return range(run * RUN, (run + 1) * RUN)

        def h_turned_of(run):
            return h_turned[:, run * RUN : (run + 1) * RUN, :]

        rh_sorted = keep.tile([P, B_TILES, PACK, P], BF16)
        rh = {}

        def reset_gates(run):
            r = work.tile([P, RUN, BATCH], F32, tag="gate")
            for k, j in enumerate(tiles_of(run)):
                acc = gate_tile(R, j, H_SUM)
                nc.scalar.activation(
                    out=r[:, k, :], in_=acc[:], func=ACT.Sigmoid, bias=bias_of(R, j), scale=1.0
                )
            rh[run] = work.tile([P, RUN, BATCH], F32, name="rh", tag="lagged", bufs=LAG + 2)
            multiplier = nc.gpsimd if run % 2 and run > 1 else nc.vector
            multiplier.tensor_tensor(out=rh[run][:], in0=r[:], in1=h_turned_of(run), op=ALU.mult)

        def sum_rh(run):
            for k, j in enumerate(tiles_of(run)):
                back = psum_turn.tile([P, B_TILES, P], F32, tag="turn")
                for i in range(B_TILES):
                    nc.tensor.transpose(back[:, i, :], rh[run][:, k, i * P : (i + 1) * P], ident_f32[:])
                units = TILE_UNITS // PACK
                with nc.allow_low_precision(reason="r_h is rounded once to bfloat16, as the task says"):
                    nc.vector.tensor_reduce(
                        out=rh_sorted[:, :, :, j * units : (j + 1) * units],
                        in_=back[:].rearrange("b i (q t m) -> b i t q m", t=PACK, m=SCALES),
                        axis=AXIS.X,
                        op=ALU.add,
                    )

        for run in range(0, RUNS, 2):
            reset_gates(run)
            reset_gates(run + 1)
            if run >= LAG:
                sum_rh(run - LAG)
                sum_rh(run - LAG + 1)

        z = [keep.tile([P, RUN, BATCH], F32, name="z%d" % run) for run in range(RUNS)]
        minus_kept = [keep.tile([P, RUN, BATCH], F32, name="minus_kept%d" % run) for run in range(RUNS)]

        def adds_on_vector(run):
            return run == 1

        def update_gates(run):
            for k, j in enumerate(tiles_of(run)):
                acc = gate_tile(Z, j, H_SUM)
                nc.scalar.activation(
                    out=z[run][:, k, :], in_=acc[:], func=ACT.Sigmoid, bias=bias_of(Z, j), scale=1.0
                )
            if adds_on_vector(run):
                return
            nc.vector.scalar_tensor_tensor(
                out=minus_kept[run][:],
                in0=z[run][:],
                scalar=1.0,
                in1=h_turned_of(run),
                op0=ALU.subtract,
                op1=ALU.mult,
            )

        for run in range(RUNS):
            update_gates(run)
            if run == LAG - 1:
                sum_rh(RUNS - LAG)
                sum_rh(RUNS - 1)
            if run == RH_READY:
                rh_grouped = work.tile([P, BATCH, PACK], BF16, tag="grouped", bufs=2, align_bytes=64)
                for i in range(B_TILES):
                    group_sorted(rh_sorted, rh_grouped, i, either_engine(i))
                quantise(rh_grouped, R_H)

        new_state = out_1.rearrange("(i b) c -> b i c", b=P)
        output = out_0.rearrange("(i b) n -> b i n", b=P)
        minus_fresh = {}
        out_halves = {}

        def candidates(run):
            h_hat = work.tile([P, RUN, BATCH], F32, tag="gate")
            for k, j in enumerate(tiles_of(run)):
                acc = gate_tile(H, j, R_H)
                nc.scalar.activation(
                    out=h_hat[:, k, :], in_=acc[:], func=ACT.Tanh, bias=bias_of(H, j), scale=1.0
                )
            minus_fresh[run] = work.tile([P, RUN, BATCH], F32, name="minus_fresh", tag="lagged", bufs=LAG + 2)
            if adds_on_vector(run):
                nc.vector.scalar_tensor_tensor(
                    out=minus_fresh[run][:],
                    in0=h_hat[:],
                    scalar=minus_alpha[:, 0:1],
                    in1=h_turned_of(run),
                    op0=ALU.mult,
                    op1=ALU.add,
                )
                return
            for tiles in pieces_of(RUN, RUN if run == RUNS - 1 else 1):
                nc.vector.scalar_tensor_tensor(
                    out=minus_fresh[run][:, tiles, :],
                    in0=z[run][:, tiles, :],
                    scalar=minus_alpha[:, 0:1],
                    in1=h_hat[:, tiles, :],
                    op0=ALU.mult,
                    op1=ALU.mult,
                )

        def weigh(run):
            if adds_on_vector(run):
                nc.vector.tensor_mul(out=minus_fresh[run][:], in0=z[run][:], in1=minus_fresh[run][:])

        def send_back(run):
            state_out = work.tile([P, B_TILES, RUN * P], F32, tag="state_out")
            out_halves[run] = work.tile([P, B_TILES, RUN * TILE_UNITS, 2], F32, name="out_halves", tag="out_halves")
            for k in range(RUN):
                back = psum_turn.tile([P, B_TILES, P], F32, tag="turn")
                for i in range(B_TILES):
                    rows = slice(i * P, (i + 1) * P)
                    terms = [minus_fresh] if adds_on_vector(run) else [minus_kept, minus_fresh]
                    for term in terms:
                        nc.tensor.matmul(
                            out=back[:, i, :], lhsT=term[run][:, k, rows], rhs=ident_f32[:],
                            is_transpose=True, start=(term is terms[0]), stop=(term is minus_fresh),
                        )
                if adds_on_vector(run):
                    nc.vector.tensor_sub(
                        out=state_out[:, :, k * P : (k + 1) * P],
                        in0=h_all[:, :, (run * RUN + k) * P : (run * RUN + k + 1) * P],
                        in1=back[:],
                    )
                else:
                    nc.scalar.mul(out=state_out[:, :, k * P : (k + 1) * P], in_=back[:], mul=-1.0)
                if run == RUNS - 1:
                    finish(run, state_out, k, 1)
            if run < RUNS - 1:
                finish(run, state_out, 0, RUN)

        def finish(run, state_out, k, tiles):
            cols = slice(k * P, (k + tiles) * P)
            nc.sync.dma_start(
                out=new_state[:, :, (run * RUN + k) * P : (run * RUN + k + tiles) * P],
                in_=state_out[:, :, cols],
            )
            by_scale = state_out[:, :, cols].rearrange("b i (n m) -> b i n m", m=SCALES)
            nc.vector.tensor_add(
                out=out_halves[run][:, :, k * TILE_UNITS : (k + tiles) * TILE_UNITS, :],
                in0=by_scale[:, :, :, 0:2],
                in1=by_scale[:, :, :, 2:4],
            )

        def sum_output(run):
            output_out = work.tile([P, B_TILES, RUN * TILE_UNITS], F32, tag="output_out", bufs=4)
            nc.vector.tensor_add(
                out=output_out[:], in0=out_halves[run][:, :, :, 0], in1=out_halves[run][:, :, :, 1]
            )
            nc.sync.dma_start(
                out=output[:, :, run * RUN * TILE_UNITS : (run + 1) * RUN * TILE_UNITS], in_=output_out[:]
            )

        for run in range(0, RUNS + LAG, 2):
            if run < RUNS:
                candidates(run)
                candidates(run + 1)
            if run >= LAG:
                send_back(run - LAG)
            if run < RUNS:
                weigh(run)
                weigh(run + 1)
            if run >= LAG:
                send_back(run - LAG + 1)
                sum_output(run - LAG)
                sum_output(run - LAG + 1)
